import numpy as np
import ml_dtypes


def mxq(x, axis, fmt="e4m3"):
    dtype, down = {"e4m3": (ml_dtypes.float8_e4m3fn, 7), "e5m2": (ml_dtypes.float8_e5m2, 14)}[fmt]
    v = np.moveaxis(np.asarray(x, np.float32).astype(ml_dtypes.bfloat16).astype(np.float64), axis, -1)
    blocks = v.reshape(v.shape[:-1] + (-1, 32))
    amax = np.abs(blocks).max(-1, keepdims=True)
    byte = np.maximum(np.where(amax > 0, np.frexp(amax)[1] - 1 + 127, 0) - down, 1)
    scale = np.exp2(byte - 127.0)
    codes = (blocks / scale).astype(np.float32).astype(dtype).astype(np.float64)
    return np.moveaxis((codes * scale).reshape(v.shape), -1, axis)


WIDE = False


def mx_kscale(k):
    if not WIDE:
        return np.ones(k)
    levels = np.array([10, -10, 5, -5, 0])
    if k % 512:
        return np.exp2(np.random.permutation(np.resize(levels, k // 32))).repeat(32)
    a = np.empty((k // 512, 16))
    for p in range(k // 512):
        a[p, :8] = np.random.permutation(np.resize(levels, 8))
        for g in range(8):
            far = levels[np.abs(levels - a[p, g]) >= 10]
            a[p, g + 8] = far[np.random.randint(len(far))]
    return np.exp2(a.ravel()).repeat(32)


BF16 = ml_dtypes.bfloat16


def bf(x):
    return np.asarray(x, np.float32).astype(BF16)


def f64(x):
    return np.asarray(x).astype(np.float64)


B, T, C, H = 4, 128, 2048, 32
HD = C // H


def rotary_pos_emb(v):
    exponents = f64(np.arange(0, HD, 2)[: HD // 2] // HD)
    freqs = 1.0 / np.power(1000.0, exponents)
    theta = f64(np.arange(T))[:, None] * freqs[None, :]
    cos = np.cos(theta)[None, :, None, :]
    sin = np.sin(theta)[None, :, None, :]
    vr = v.reshape(B, T, H, HD // 2, 2)
    v0, v1 = vr[..., 0], vr[..., 1]
    out = np.stack([v0 * cos - v1 * sin, v0 * sin + v1 * cos], axis=-1)
    return out.reshape(B, T, H, HD)


def setup_inputs():
    s = mx_kscale(C)
    return {"x": bf(np.random.standard_normal((B, T, C)) * s),
            "wq": bf(np.random.standard_normal((C, C)) / np.sqrt(C) / s[None, :]),
            "wk": bf(np.random.standard_normal((C, C)) / np.sqrt(C) / s[None, :])}


def reference(x, wq, wk):
    xm = mxq(f64(x), 2, "e4m3")
    q = (xm @ mxq(f64(wq), 1, "e4m3").T).reshape(B, T, H, HD)
    k = (xm @ mxq(f64(wk), 1, "e4m3").T).reshape(B, T, H, HD)
    return rotary_pos_emb(q), rotary_pos_emb(k)

@@ -1,0 +1,196 @@
+import math
+from contextlib import ExitStack
+
+import concourse.mybir as mybir
+from concourse.masks import make_identity
+
+F32 = mybir.dt.float32
+BF16 = mybir.dt.bfloat16
+I32 = mybir.dt.int32
+U32 = mybir.dt.uint32
+U8 = mybir.dt.uint8
+FP8X4 = mybir.dt.float8_e4m3fn_x4
+ALU = mybir.AluOpType
+ACT = mybir.ActivationFunctionType
+
+P = 128
+BATCHES = 4
+CHANNELS = 2048
+PACK = 4
+PASSES = CHANNELS // (P * PACK)
+GROUP_ROWS = 512
+HALF_ROWS = GROUP_ROWS // 2
+BLOCKS = GROUP_ROWS // P
+GROUPS_PER_WEIGHT = CHANNELS // GROUP_ROWS
+WEIGHT_GROUPS = 2 * GROUPS_PER_WEIGHT
+LOADS_AHEAD = 4
+
+FLOPS = 2 * (BATCHES * P) * CHANNELS * (2 * CHANNELS)
+
+TWO_PI = 2.0 * math.pi
+TWO_PI_HIGH = 6.28125
+TWO_PI_MID = int((TWO_PI - TWO_PI_HIGH) * 2**25) / 2**25
+TWO_PI_LOW = TWO_PI - TWO_PI_HIGH - TWO_PI_MID
+HALF_PI_HIGH = int(0.5 * math.pi * 2**20) / 2**20
+HALF_PI_LOW = 0.5 * math.pi - HALF_PI_HIGH
+ROUND_TO_WHOLE = 1.5 * 2**23
+
+
+def position_trig(nc, pool):
+    position_int = pool.tile([P, 1], I32, name="position_int")
+    nc.gpsimd.iota(position_int[:], pattern=[[0, 1]], base=0, channel_multiplier=1)
+    position = pool.tile([P, 1], F32, name="position")
+    nc.vector.tensor_copy(out=position[:], in_=position_int[:])
+
+    shifted = pool.tile([P, 1], F32, name="shifted")
+    nc.vector.tensor_scalar(
+        out=shifted[:], in0=position[:], scalar1=1.0 / TWO_PI, scalar2=ROUND_TO_WHOLE, op0=ALU.mult, op1=ALU.add
+    )
+    turns = pool.tile([P, 1], F32, name="turns")
+    nc.vector.tensor_scalar(out=turns[:], in0=shifted[:], scalar1=ROUND_TO_WHOLE, scalar2=None, op0=ALU.subtract)
+
+    angles = pool.tile([P, 2], F32, name="angles")
+    less_high = pool.tile([P, 1], F32, name="less_high")
+    less_mid = pool.tile([P, 1], F32, name="less_mid")
+    nc.vector.scalar_tensor_tensor(
+        out=less_high[:], in0=turns[:], scalar=-TWO_PI_HIGH, in1=position[:], op0=ALU.mult, op1=ALU.add
+    )
+    nc.vector.scalar_tensor_tensor(
+        out=less_mid[:], in0=turns[:], scalar=-TWO_PI_MID, in1=less_high[:], op0=ALU.mult, op1=ALU.add
+    )
+    nc.vector.scalar_tensor_tensor(
+        out=angles[:, 0:1], in0=turns[:], scalar=-TWO_PI_LOW, in1=less_mid[:], op0=ALU.mult, op1=ALU.add
+    )
+    magnitude = pool.tile([P, 1], F32, name="magnitude")
+    nc.vector.scalar_tensor_tensor(
+        out=magnitude[:], in0=angles[:, 0:1], scalar=-1.0, in1=angles[:, 0:1], op0=ALU.mult, op1=ALU.max
+    )
+    nc.vector.tensor_scalar(
+        out=angles[:, 1:2],
+        in0=magnitude[:],
+        scalar1=HALF_PI_HIGH,
+        scalar2=HALF_PI_LOW,
+        op0=ALU.subtract,
+        op1=ALU.subtract,
+    )
+
+    sines = pool.tile([P, 2], F32, name="sines")
+    nc.scalar.activation(out=sines[:], in_=angles[:], func=ACT.Sin)
+    negated = pool.tile([P, 2], F32, name="negated")
+    nc.vector.tensor_scalar(out=negated[:], in0=sines[:], scalar1=-1.0, scalar2=None, op0=ALU.mult)
+    return sines[:, 0:1], negated[:, 0:1], negated[:, 1:2]
+
+
+def tile_attention_pa_kernel(tc, x, wq, wk, out_0, out_1):
+    nc = tc.nc
+
+    group_halves = [[x[2 * half : 2 * half + 2].rearrange("b t k -> t b k") for half in range(2)]]
+    for weight in (wq, wk):
+        for c in range(GROUPS_PER_WEIGHT):
+            rows = weight[c * GROUP_ROWS : (c + 1) * GROUP_ROWS, :]
+            by_parity = rows.rearrange("(h r two) k -> two r h k", h=2, two=2)
+            group_halves.append([by_parity[two] for two in range(2)])
+
+    outputs = [out.rearrange("b t h d -> b t (h d)") for out in (out_0, out_1)]
+
+    with ExitStack() as stack:
+        const = stack.enter_context(tc.tile_pool(name="const", bufs=1))
+        raw_pool = stack.enter_context(tc.tile_pool(name="raw", bufs=LOADS_AHEAD + 1))
+        grouped_pool = stack.enter_context(tc.tile_pool(name="grouped", bufs=2 * PASSES))
+        weight_mx = stack.enter_context(tc.tile_pool(name="weight_mx", bufs=3))
+        crossed_pool = stack.enter_context(tc.tile_pool(name="crossed", bufs=4))
+        rotated_pool = stack.enter_context(tc.tile_pool(name="rotated", bufs=6))
+        transposed_pool = stack.enter_context(tc.psum_pool(name="transposed", bufs=4))
+        acc_pool = stack.enter_context(tc.psum_pool(name="acc", bufs=4))
+        stack.enter_context(tc.manual_schedule())
+
+        raw_tiles = {}
+
+        def start_load(n):
+            raw = raw_pool.tile([P, BLOCKS, CHANNELS], BF16, name="raw")
+            for half in range(2):
+                nc.sync.dma_start(out=raw[:, 2 * half : 2 * half + 2, :], in_=group_halves[n][half])
+            raw_tiles[n] = raw
+
+        def quantise_half(n, half, codes, scales):
+            raw_words = raw_tiles[n][:].bitcast(F32)
+            columns = slice(half * HALF_ROWS, (half + 1) * HALF_ROWS)
+            grouped_tiles = []
+            for g in range(PASSES):
+                bank = transposed_pool.tile([P, 2, 2, P], F32, name="bank")
+                for u in range(2):
+                    for j in range(2):
+                        nc.tensor.transpose(
+                            out=bank[:, u, j, :],
+                            in_=raw_words[:, 2 * half + j, 2 * P * g + u : 2 * P * (g + 1) : 2],
+                            identity=identity[:],
+                        )
+                grouped = grouped_pool.tile([P, HALF_ROWS, PACK], BF16, name="grouped", align_bytes=64)
+                copy_out = nc.vector.tensor_copy if g == PASSES - 1 else nc.scalar.copy
+                copy_out(out=grouped[:].bitcast(F32), in_=bank[:].rearrange("p u j r -> p (j r) u"))
+                grouped_tiles.append(grouped)
+            for g in range(PASSES):
+                nc.vector.quantize_mx(
+                    out=codes[:, g, columns].bitcast(FP8X4),
+                    scales=scales[:, g, columns],
+                    in_=grouped_tiles[g][:].rearrange("p n t -> p (n t)"),
+                )
+
+        def project_and_rotate(c, b, w_codes, w_scales):
+            tokens = slice(b * P, (b + 1) * P)
+            acc = acc_pool.tile([P, GROUP_ROWS], F32, name="acc")
+            for g in range(PASSES):
+                nc.tensor.matmul_mx(
+                    out=acc[:],
+                    lhsT=x_codes[:, g, tokens].bitcast(FP8X4),
+                    lhsT_scale=x_scales[:, g, tokens],
+                    rhs=w_codes[:, g, :].bitcast(FP8X4),
+                    rhs_scale=w_scales[:, g, :],
+                    start=(g == 0),
+                    stop=(g == PASSES - 1),
+                )
+            crossed = crossed_pool.tile([P, GROUP_ROWS], F32, name="crossed")
+            nc.scalar.activation(out=crossed[:, :HALF_ROWS], in_=acc[:, HALF_ROWS:], func=ACT.Copy, scale=minus_sin_t)
+            nc.scalar.activation(out=crossed[:, HALF_ROWS:], in_=acc[:, :HALF_ROWS], func=ACT.Copy, scale=sin_t)
+            rotated = rotated_pool.tile([P, HALF_ROWS, 2], F32, name="rotated")
+            nc.vector.scalar_tensor_tensor(
+                out=rotated[:],
+                in0=acc[:].rearrange("p (two i) -> p i two", two=2),
+                scalar=cos_t,
+                in1=crossed[:].rearrange("p (two i) -> p i two", two=2),
+                op0=ALU.mult,
+                op1=ALU.add,
+            )
+            first_channel = (c % GROUPS_PER_WEIGHT) * GROUP_ROWS
+            nc.sync.dma_start(
+                out=outputs[c // GROUPS_PER_WEIGHT][b, :, first_channel : first_channel + GROUP_ROWS],
+                in_=rotated[:].rearrange("p i two -> p (i two)"),
+            )
+
+        for n in range(LOADS_AHEAD):
+            start_load(n)
+
+        identity = const.tile([P, P], F32, name="identity")
+        make_identity(nc, identity[:])
+
+        sin_t, minus_sin_t, cos_t = position_trig(nc, const)
+
+        x_codes = const.tile([P, PASSES, GROUP_ROWS], U32, name="x_codes", align_bytes=64)
+        x_scales = const.tile([P, PASSES, GROUP_ROWS], U8, name="x_scales", align_bytes=64)
+        for half in range(2):
+            quantise_half(0, half, x_codes, x_scales)
+
+        prepared = {}
+        for c in range(WEIGHT_GROUPS + 1):
+            if c + LOADS_AHEAD <= WEIGHT_GROUPS:
+                start_load(c + LOADS_AHEAD)
+            if c < WEIGHT_GROUPS:
+                w_codes = weight_mx.tile([P, PASSES, GROUP_ROWS], U32, name="w_codes", align_bytes=64)
+                w_scales = weight_mx.tile([P, PASSES, GROUP_ROWS], U8, name="w_scales", align_bytes=64)
+                prepared[c] = (w_codes, w_scales)
+            for half in range(2):
+                if c < WEIGHT_GROUPS:
+                    quantise_half(c + 1, half, prepared[c][0], prepared[c][1])
+                if c > 0:
+                    for b in (2 * half, 2 * half + 1):
+                        project_and_rotate(c - 1, b, prepared[c - 1][0], prepared[c - 1][1])

@@ -23,6 +23,7 @@ HALF_ROWS = GROUP_ROWS // 2
 BLOCKS = GROUP_ROWS // P
 GROUPS_PER_WEIGHT = CHANNELS // GROUP_ROWS
 WEIGHT_GROUPS = 2 * GROUPS_PER_WEIGHT
+RUN = 16
 LOADS_AHEAD = 4
 
 FLOPS = 2 * (BATCHES * P) * CHANNELS * (2 * CHANNELS)
@@ -96,6 +97,7 @@ def tile_attention_pa_kernel(tc, x, wq, wk, out_0, out_1):
     with ExitStack() as stack:
         const = stack.enter_context(tc.tile_pool(name="const", bufs=1))
         raw_pool = stack.enter_context(tc.tile_pool(name="raw", bufs=LOADS_AHEAD + 1))
+        sorted_pool = stack.enter_context(tc.tile_pool(name="sorted", bufs=3))
         grouped_pool = stack.enter_context(tc.tile_pool(name="grouped", bufs=2 * PASSES))
         weight_mx = stack.enter_context(tc.tile_pool(name="weight_mx", bufs=3))
         crossed_pool = stack.enter_context(tc.tile_pool(name="crossed", bufs=4))
@@ -112,22 +114,32 @@ def tile_attention_pa_kernel(tc, x, wq, wk, out_0, out_1):
                 nc.sync.dma_start(out=raw[:, 2 * half : 2 * half + 2, :], in_=group_halves[n][half])
             raw_tiles[n] = raw
 
+        sorted_tiles = {}
+
+        def sort_half(n, half):
+            planes = sorted_pool.tile([P, 2, 2, CHANNELS // 2], BF16, name="planes")
+            nc.vector.tensor_copy(
+                out=planes[:].rearrange("p u j (r i) -> p u (j r) i", i=RUN),
+                in_=raw_tiles[n][:, 2 * half : 2 * half + 2, :].rearrange("p j (r u i) -> p u (j r) i", u=2, i=RUN),
+            )
+            sorted_tiles[n, half] = planes
+
         def quantise_half(n, half, codes, scales):
-            raw_words = raw_tiles[n][:].bitcast(F32)
+            words = sorted_tiles[n, half][:].rearrange("p u j k -> p (u j k)").bitcast(F32)
             columns = slice(half * HALF_ROWS, (half + 1) * HALF_ROWS)
             grouped_tiles = []
             for g in range(PASSES):
                 bank = transposed_pool.tile([P, 2, 2, P], F32, name="bank")
                 for u in range(2):
                     for j in range(2):
+                        first_word = ((2 * u + j) * PASSES + g) * P
                         nc.tensor.transpose(
                             out=bank[:, u, j, :],
-                            in_=raw_words[:, 2 * half + j, 2 * P * g + u : 2 * P * (g + 1) : 2],
+                            in_=words[:, first_word : first_word + P],
                             identity=identity[:],
                         )
                 grouped = grouped_pool.tile([P, HALF_ROWS, PACK], BF16, name="grouped", align_bytes=64)
-                copy_out = nc.vector.tensor_copy if g == PASSES - 1 else nc.scalar.copy
-                copy_out(out=grouped[:].bitcast(F32), in_=bank[:].rearrange("p u j r -> p (j r) u"))
+                nc.scalar.copy(out=grouped[:].bitcast(F32), in_=bank[:].rearrange("p u j r -> p (j r) u"))
                 grouped_tiles.append(grouped)
             for g in range(PASSES):
                 nc.vector.quantize_mx(
@@ -177,7 +189,10 @@ def tile_attention_pa_kernel(tc, x, wq, wk, out_0, out_1):
 
         x_codes = const.tile([P, PASSES, GROUP_ROWS], U32, name="x_codes", align_bytes=64)
         x_scales = const.tile([P, PASSES, GROUP_ROWS], U8, name="x_scales", align_bytes=64)
+        units = [(n, half) for n in range(WEIGHT_GROUPS + 1) for half in range(2)]
+        sort_half(*units[0])
         for half in range(2):
+            sort_half(*units[half + 1])
             quantise_half(0, half, x_codes, x_scales)
 
         prepared = {}
@@ -190,6 +205,8 @@ def tile_attention_pa_kernel(tc, x, wq, wk, out_0, out_1):
                 prepared[c] = (w_codes, w_scales)
             for half in range(2):
                 if c < WEIGHT_GROUPS:
+                    if 2 * c + half + 3 < len(units):
+                        sort_half(*units[2 * c + half + 3])
                     quantise_half(c + 1, half, prepared[c][0], prepared[c][1])
                 if c > 0:
                     for b in (2 * half, 2 * half + 1):

@@ -23,7 +23,6 @@ HALF_ROWS = GROUP_ROWS // 2
 BLOCKS = GROUP_ROWS // P
 GROUPS_PER_WEIGHT = CHANNELS // GROUP_ROWS
 WEIGHT_GROUPS = 2 * GROUPS_PER_WEIGHT
-RUN = 16
 LOADS_AHEAD = 4
 
 FLOPS = 2 * (BATCHES * P) * CHANNELS * (2 * CHANNELS)
@@ -119,23 +118,27 @@ def tile_attention_pa_kernel(tc, x, wq, wk, out_0, out_1):
         def sort_half(n, half):
             planes = sorted_pool.tile([P, 2, 2, CHANNELS // 2], BF16, name="planes")
             nc.vector.tensor_copy(
-                out=planes[:].rearrange("p u j (r i) -> p u (j r) i", i=RUN),
-                in_=raw_tiles[n][:, 2 * half : 2 * half + 2, :].rearrange("p j (r u i) -> p u (j r) i", u=2, i=RUN),
+                out=planes[:].rearrange("p u j (w e) -> p u (j w) e", e=2),
+                in_=raw_tiles[n][:, 2 * half : 2 * half + 2, :].rearrange("p j (w u e) -> p u (j w) e", u=2, e=2),
             )
             sorted_tiles[n, half] = planes
 
         def quantise_half(n, half, codes, scales):
-            words = sorted_tiles[n, half][:].rearrange("p u j k -> p (u j k)").bitcast(F32)
+            if n == 0:
+                raw_words = raw_tiles[n][:].bitcast(F32)
+                words = [[raw_words[:, 2 * half + j, u::2] for j in range(2)] for u in range(2)]
+            else:
+                planes = sorted_tiles[n, half][:].rearrange("p u j k -> p (u j) k").bitcast(F32)
+                words = [[planes[:, 2 * u + j, :] for j in range(2)] for u in range(2)]
             columns = slice(half * HALF_ROWS, (half + 1) * HALF_ROWS)
             grouped_tiles = []
             for g in range(PASSES):
                 bank = transposed_pool.tile([P, 2, 2, P], F32, name="bank")
                 for u in range(2):
                     for j in range(2):
-                        first_word = ((2 * u + j) * PASSES + g) * P
                         nc.tensor.transpose(
                             out=bank[:, u, j, :],
-                            in_=words[:, first_word : first_word + P],
+                            in_=words[u][j][:, g * P : (g + 1) * P],
                             identity=identity[:],
                         )
                 grouped = grouped_pool.tile([P, HALF_ROWS, PACK], BF16, name="grouped", align_bytes=64)
@@ -190,10 +193,9 @@ def tile_attention_pa_kernel(tc, x, wq, wk, out_0, out_1):
         x_codes = const.tile([P, PASSES, GROUP_ROWS], U32, name="x_codes", align_bytes=64)
         x_scales = const.tile([P, PASSES, GROUP_ROWS], U8, name="x_scales", align_bytes=64)
         units = [(n, half) for n in range(WEIGHT_GROUPS + 1) for half in range(2)]
-        sort_half(*units[0])
         for half in range(2):
-            sort_half(*units[half + 1])
             quantise_half(0, half, x_codes, x_scales)
+        sort_half(*units[2])
 
         prepared = {}
         for c in range(WEIGHT_GROUPS + 1):

@@ -19,11 +19,11 @@ CHANNELS = 2048
 PACK = 4
 PASSES = CHANNELS // (P * PACK)
 GROUP_ROWS = 512
-HALF_ROWS = GROUP_ROWS // 2
-BLOCKS = GROUP_ROWS // P
+UNIT_ROWS = GROUP_ROWS // 2
+UNIT_BLOCKS = UNIT_ROWS // P
 GROUPS_PER_WEIGHT = CHANNELS // GROUP_ROWS
 WEIGHT_GROUPS = 2 * GROUPS_PER_WEIGHT
-LOADS_AHEAD = 4
+LOADS_AHEAD = 6
 
 FLOPS = 2 * (BATCHES * P) * CHANNELS * (2 * CHANNELS)
 
@@ -84,18 +84,21 @@ def position_trig(nc, pool):
 def tile_attention_pa_kernel(tc, x, wq, wk, out_0, out_1):
     nc = tc.nc
 
-    group_halves = [[x[2 * half : 2 * half + 2].rearrange("b t k -> t b k") for half in range(2)]]
-    for weight in (wq, wk):
-        for c in range(GROUPS_PER_WEIGHT):
-            rows = weight[c * GROUP_ROWS : (c + 1) * GROUP_ROWS, :]
-            by_parity = rows.rearrange("(h r two) k -> two r h k", h=2, two=2)
-            group_halves.append([by_parity[two] for two in range(2)])
+    unit_views = {}
+    for c in range(WEIGHT_GROUPS):
+        first_row = (c % GROUPS_PER_WEIGHT) * GROUP_ROWS
+        rows = (wq, wk)[c // GROUPS_PER_WEIGHT][first_row : first_row + GROUP_ROWS, :]
+        by_parity = rows.rearrange("(h r two) k -> two r h k", h=UNIT_BLOCKS, two=2)
+        for two in range(2):
+            unit_views[c, two] = by_parity[two]
+    streamed_units = [unit for unit in unit_views if unit[0] > 0]
 
     outputs = [out.rearrange("b t h d -> b t (h d)") for out in (out_0, out_1)]
 
     with ExitStack() as stack:
         const = stack.enter_context(tc.tile_pool(name="const", bufs=1))
-        raw_pool = stack.enter_context(tc.tile_pool(name="raw", bufs=LOADS_AHEAD + 1))
+        block_pool = stack.enter_context(tc.tile_pool(name="block", bufs=BATCHES + GROUP_ROWS // P))
+        unit_pool = stack.enter_context(tc.tile_pool(name="unit", bufs=LOADS_AHEAD + 1))
         sorted_pool = stack.enter_context(tc.tile_pool(name="sorted", bufs=3))
         grouped_pool = stack.enter_context(tc.tile_pool(name="grouped", bufs=2 * PASSES))
         weight_mx = stack.enter_context(tc.tile_pool(name="weight_mx", bufs=3))
@@ -105,32 +108,58 @@ def tile_attention_pa_kernel(tc, x, wq, wk, out_0, out_1):
         acc_pool = stack.enter_context(tc.psum_pool(name="acc", bufs=4))
         stack.enter_context(tc.manual_schedule())
 
-        raw_tiles = {}
-
-        def start_load(n):
-            raw = raw_pool.tile([P, BLOCKS, CHANNELS], BF16, name="raw")
-            for half in range(2):
-                nc.sync.dma_start(out=raw[:, 2 * half : 2 * half + 2, :], in_=group_halves[n][half])
-            raw_tiles[n] = raw
-
+        unit_tiles = {}
         sorted_tiles = {}
+        prepared = {}
 
-        def sort_half(n, half):
+        def load_block(view):
+            block = block_pool.tile([P, CHANNELS], BF16, name="block")
+            nc.sync.dma_start(out=block[:], in_=view)
+            return block
+
+        def start_load(unit):
+            raw = unit_pool.tile([P, UNIT_BLOCKS, CHANNELS], BF16, name="raw")
+            nc.sync.dma_start(out=raw[:], in_=unit_views[unit])
+            unit_tiles[unit] = raw
+
+        def codes_of_group(c):
+            if c not in prepared:
+                w_codes = weight_mx.tile([P, PASSES, GROUP_ROWS], U32, name="w_codes", align_bytes=64)
+                w_scales = weight_mx.tile([P, PASSES, GROUP_ROWS], U8, name="w_scales", align_bytes=64)
+                prepared[c] = (w_codes, w_scales)
+            return prepared[c]
+
+        def regroup_block(block, copy_engines):
+            words = block[:].bitcast(F32)
+            grouped_tiles = []
+            for pair in range(PASSES // 2):
+                bank = transposed_pool.tile([P, 2, 2, P], F32, name="bank")
+                for e in range(2):
+                    first_word = (2 * pair + e) * 2 * P
+                    for u in range(2):
+                        nc.tensor.transpose(
+                            out=bank[:, e, u, :],
+                            in_=words[:, first_word + u : first_word + 2 * P : 2],
+                            identity=identity[:],
+                        )
+                grouped = grouped_pool.tile([P, 2, P, PACK], BF16, name="grouped", align_bytes=64)
+                copy_engines[pair](out=grouped[:].bitcast(F32), in_=bank[:].rearrange("p e u r -> p e r u"))
+                grouped_tiles.append(grouped)
+            return grouped_tiles
+
+        def sort_unit(unit):
             planes = sorted_pool.tile([P, 2, 2, CHANNELS // 2], BF16, name="planes")
             nc.vector.tensor_copy(
                 out=planes[:].rearrange("p u j (w e) -> p u (j w) e", e=2),
-                in_=raw_tiles[n][:, 2 * half : 2 * half + 2, :].rearrange("p j (w u e) -> p u (j w) e", u=2, e=2),
+                in_=unit_tiles[unit][:].rearrange("p j (w u e) -> p u (j w) e", u=2, e=2),
             )
-            sorted_tiles[n, half] = planes
+            sorted_tiles[unit] = planes
 
-        def quantise_half(n, half, codes, scales):
-            if n == 0:
-                raw_words = raw_tiles[n][:].bitcast(F32)
-                words = [[raw_words[:, 2 * half + j, u::2] for j in range(2)] for u in range(2)]
-            else:
-                planes = sorted_tiles[n, half][:].rearrange("p u j k -> p (u j) k").bitcast(F32)
-                words = [[planes[:, 2 * u + j, :] for j in range(2)] for u in range(2)]
-            columns = slice(half * HALF_ROWS, (half + 1) * HALF_ROWS)
+        def quantise_unit(unit):
+            c, two = unit
+            codes, scales = codes_of_group(c)
+            columns = slice(two * UNIT_ROWS, (two + 1) * UNIT_ROWS)
+            planes = sorted_tiles[unit][:].rearrange("p u j k -> p (u j) k").bitcast(F32)
             grouped_tiles = []
             for g in range(PASSES):
                 bank = transposed_pool.tile([P, 2, 2, P], F32, name="bank")
@@ -138,10 +167,10 @@ def tile_attention_pa_kernel(tc, x, wq, wk, out_0, out_1):
                     for j in range(2):
                         nc.tensor.transpose(
                             out=bank[:, u, j, :],
-                            in_=words[u][j][:, g * P : (g + 1) * P],
+                            in_=planes[:, 2 * u + j, g * P : (g + 1) * P],
                             identity=identity[:],
                         )
-                grouped = grouped_pool.tile([P, HALF_ROWS, PACK], BF16, name="grouped", align_bytes=64)
+                grouped = grouped_pool.tile([P, UNIT_ROWS, PACK], BF16, name="grouped", align_bytes=64)
                 nc.scalar.copy(out=grouped[:].bitcast(F32), in_=bank[:].rearrange("p u j r -> p (j r) u"))
                 grouped_tiles.append(grouped)
             for g in range(PASSES):
@@ -151,23 +180,24 @@ def tile_attention_pa_kernel(tc, x, wq, wk, out_0, out_1):
                     in_=grouped_tiles[g][:].rearrange("p n t -> p (n t)"),
                 )
 
-        def project_and_rotate(c, b, w_codes, w_scales):
-            tokens = slice(b * P, (b + 1) * P)
+        def project_and_rotate(c, b):
+            w_codes, w_scales = prepared[c]
             acc = acc_pool.tile([P, GROUP_ROWS], F32, name="acc")
             for g in range(PASSES):
                 nc.tensor.matmul_mx(
                     out=acc[:],
-                    lhsT=x_codes[:, g, tokens].bitcast(FP8X4),
-                    lhsT_scale=x_scales[:, g, tokens],
+                    lhsT=x_codes[:, b, g, :].bitcast(FP8X4),
+                    lhsT_scale=x_scales[:, b, g, :],
                     rhs=w_codes[:, g, :].bitcast(FP8X4),
                     rhs_scale=w_scales[:, g, :],
                     start=(g == 0),
                     stop=(g == PASSES - 1),
                 )
             crossed = crossed_pool.tile([P, GROUP_ROWS], F32, name="crossed")
-            nc.scalar.activation(out=crossed[:, :HALF_ROWS], in_=acc[:, HALF_ROWS:], func=ACT.Copy, scale=minus_sin_t)
-            nc.scalar.activation(out=crossed[:, HALF_ROWS:], in_=acc[:, :HALF_ROWS], func=ACT.Copy, scale=sin_t)
-            rotated = rotated_pool.tile([P, HALF_ROWS, 2], F32, name="rotated")
+            even, odd = slice(0, UNIT_ROWS), slice(UNIT_ROWS, GROUP_ROWS)
+            nc.scalar.activation(out=crossed[:, even], in_=acc[:, odd], func=ACT.Copy, scale=minus_sin_t)
+            nc.scalar.activation(out=crossed[:, odd], in_=acc[:, even], func=ACT.Copy, scale=sin_t)
+            rotated = rotated_pool.tile([P, UNIT_ROWS, 2], F32, name="rotated")
             nc.vector.scalar_tensor_tensor(
                 out=rotated[:],
                 in0=acc[:].rearrange("p (two i) -> p i two", two=2),
@@ -182,34 +212,55 @@ def tile_attention_pa_kernel(tc, x, wq, wk, out_0, out_1):
                 in_=rotated[:].rearrange("p i two -> p (i two)"),
             )
 
-        for n in range(LOADS_AHEAD):
-            start_load(n)
+        x_blocks = [load_block(x[b]) for b in range(BATCHES)]
+        first_group_blocks = {}
+        for two in range(2):
+            for h in range(UNIT_BLOCKS):
+                first_group_blocks[two, h] = load_block(unit_views[0, two][:, h, :])
+        for unit in streamed_units[:LOADS_AHEAD]:
+            start_load(unit)
 
         identity = const.tile([P, P], F32, name="identity")
         make_identity(nc, identity[:])
 
         sin_t, minus_sin_t, cos_t = position_trig(nc, const)
 
-        x_codes = const.tile([P, PASSES, GROUP_ROWS], U32, name="x_codes", align_bytes=64)
-        x_scales = const.tile([P, PASSES, GROUP_ROWS], U8, name="x_scales", align_bytes=64)
-        units = [(n, half) for n in range(WEIGHT_GROUPS + 1) for half in range(2)]
-        for half in range(2):
-            quantise_half(0, half, x_codes, x_scales)
-        sort_half(*units[2])
+        x_codes = const.tile([P, BATCHES, PASSES, P], U32, name="x_codes", align_bytes=64)
+        x_scales = const.tile([P, BATCHES, PASSES, P], U8, name="x_scales", align_bytes=64)
+        for b in range(BATCHES):
+            grouped_tiles = regroup_block(x_blocks[b], (nc.scalar.copy, nc.vector.tensor_copy))
+            for pair in range(PASSES // 2):
+                passes = slice(2 * pair, 2 * pair + 2)
+                nc.vector.quantize_mx(
+                    out=x_codes[:, b, passes, :].rearrange("p g r -> p (g r)").bitcast(FP8X4),
+                    scales=x_scales[:, b, passes, :].rearrange("p g r -> p (g r)"),
+                    in_=grouped_tiles[pair][:].rearrange("p e r t -> p (e r t)"),
+                )
+        codes, scales = codes_of_group(0)
+        for two, h in first_group_blocks:
+            grouped_tiles = regroup_block(first_group_blocks[two, h], (nc.scalar.copy, nc.scalar.copy))
+            first_column = two * UNIT_ROWS + h * P
+            columns = slice(first_column, first_column + P)
+            for g in range(PASSES):
+                nc.vector.quantize_mx(
+                    out=codes[:, g, columns].bitcast(FP8X4),
+                    scales=scales[:, g, columns],
+                    in_=grouped_tiles[g // 2][:, g % 2].rearrange("p r t -> p (r t)"),
+                )
 
-        prepared = {}
-        for c in range(WEIGHT_GROUPS + 1):
-            if c + LOADS_AHEAD <= WEIGHT_GROUPS:
-                start_load(c + LOADS_AHEAD)
-            if c < WEIGHT_GROUPS:
-                w_codes = weight_mx.tile([P, PASSES, GROUP_ROWS], U32, name="w_codes", align_bytes=64)
-                w_scales = weight_mx.tile([P, PASSES, GROUP_ROWS], U8, name="w_scales", align_bytes=64)
-                prepared[c] = (w_codes, w_scales)
-            for half in range(2):
-                if c < WEIGHT_GROUPS:
-                    if 2 * c + half + 3 < len(units):
-                        sort_half(*units[2 * c + half + 3])
-                    quantise_half(c + 1, half, prepared[c][0], prepared[c][1])
-                if c > 0:
-                    for b in (2 * half, 2 * half + 1):
-                        project_and_rotate(c - 1, b, prepared[c - 1][0], prepared[c - 1][1])
+        turns = [(c, b) for c in range(WEIGHT_GROUPS) for b in range(BATCHES)]
+        project_and_rotate(*turns[0])
+        done = 1
+        sort_unit(streamed_units[0])
+        for s, unit in enumerate(streamed_units):
+            if s + LOADS_AHEAD < len(streamed_units):
+                start_load(streamed_units[s + LOADS_AHEAD])
+            if s + 1 < len(streamed_units):
+                sort_unit(streamed_units[s + 1])
+            quantise_unit(unit)
+            count = 1 if s == 1 else 2
+            for c, b in turns[done : done + count]:
+                project_and_rotate(c, b)
+            done += count
+        for c, b in turns[done:]:
+            project_and_rotate(c, b)

@@ -100,6 +100,7 @@ def tile_attention_pa_kernel(tc, x, wq, wk, out_0, out_1):
         block_pool = stack.enter_context(tc.tile_pool(name="block", bufs=BATCHES + GROUP_ROWS // P))
         unit_pool = stack.enter_context(tc.tile_pool(name="unit", bufs=LOADS_AHEAD + 1))
         sorted_pool = stack.enter_context(tc.tile_pool(name="sorted", bufs=3))
+        sorted_block_pool = stack.enter_context(tc.tile_pool(name="sorted_block", bufs=2))
         grouped_pool = stack.enter_context(tc.tile_pool(name="grouped", bufs=2 * PASSES))
         weight_mx = stack.enter_context(tc.tile_pool(name="weight_mx", bufs=3))
         crossed_pool = stack.enter_context(tc.tile_pool(name="crossed", bufs=4))
@@ -129,17 +130,28 @@ def tile_attention_pa_kernel(tc, x, wq, wk, out_0, out_1):
                 prepared[c] = (w_codes, w_scales)
             return prepared[c]
 
-        def regroup_block(block, copy_engines):
+        def unsorted_words(block):
             words = block[:].bitcast(F32)
+            return [words[:, u::2] for u in range(2)]
+
+        def sort_block(block):
+            planes = sorted_block_pool.tile([P, 2, CHANNELS // 2], BF16, name="block_planes")
+            nc.vector.tensor_copy(
+                out=planes[:].rearrange("p u (w e) -> p u w e", e=2),
+                in_=block[:].rearrange("p (w u e) -> p u w e", u=2, e=2),
+            )
+            return [planes[:, u, :].bitcast(F32) for u in range(2)]
+
+        def regroup_block(words, copy_engines):
             grouped_tiles = []
             for pair in range(PASSES // 2):
                 bank = transposed_pool.tile([P, 2, 2, P], F32, name="bank")
                 for e in range(2):
-                    first_word = (2 * pair + e) * 2 * P
+                    first_word = (2 * pair + e) * P
                     for u in range(2):
                         nc.tensor.transpose(
                             out=bank[:, e, u, :],
-                            in_=words[:, first_word + u : first_word + 2 * P : 2],
+                            in_=words[u][:, first_word : first_word + P],
                             identity=identity[:],
                         )
                 grouped = grouped_pool.tile([P, 2, P, PACK], BF16, name="grouped", align_bytes=64)
@@ -212,11 +224,11 @@ def tile_attention_pa_kernel(tc, x, wq, wk, out_0, out_1):
                 in_=rotated[:].rearrange("p i two -> p (i two)"),
             )
 
-        x_blocks = [load_block(x[b]) for b in range(BATCHES)]
         first_group_blocks = {}
         for two in range(2):
             for h in range(UNIT_BLOCKS):
                 first_group_blocks[two, h] = load_block(unit_views[0, two][:, h, :])
+        x_blocks = [load_block(x[b]) for b in range(BATCHES)]
         for unit in streamed_units[:LOADS_AHEAD]:
             start_load(unit)
 
@@ -225,20 +237,10 @@ def tile_attention_pa_kernel(tc, x, wq, wk, out_0, out_1):
 
         sin_t, minus_sin_t, cos_t = position_trig(nc, const)
 
-        x_codes = const.tile([P, BATCHES, PASSES, P], U32, name="x_codes", align_bytes=64)
-        x_scales = const.tile([P, BATCHES, PASSES, P], U8, name="x_scales", align_bytes=64)
-        for b in range(BATCHES):
-            grouped_tiles = regroup_block(x_blocks[b], (nc.scalar.copy, nc.vector.tensor_copy))
-            for pair in range(PASSES // 2):
-                passes = slice(2 * pair, 2 * pair + 2)
-                nc.vector.quantize_mx(
-                    out=x_codes[:, b, passes, :].rearrange("p g r -> p (g r)").bitcast(FP8X4),
-                    scales=x_scales[:, b, passes, :].rearrange("p g r -> p (g r)"),
-                    in_=grouped_tiles[pair][:].rearrange("p e r t -> p (e r t)"),
-                )
         codes, scales = codes_of_group(0)
         for two, h in first_group_blocks:
-            grouped_tiles = regroup_block(first_group_blocks[two, h], (nc.scalar.copy, nc.scalar.copy))
+            second_copy = nc.scalar.copy if h == 0 else nc.vector.tensor_copy
+            grouped_tiles = regroup_block(unsorted_words(first_group_blocks[two, h]), (nc.scalar.copy, second_copy))
             first_column = two * UNIT_ROWS + h * P
             columns = slice(first_column, first_column + P)
             for g in range(PASSES):
@@ -248,19 +250,36 @@ def tile_attention_pa_kernel(tc, x, wq, wk, out_0, out_1):
                     in_=grouped_tiles[g // 2][:, g % 2].rearrange("p r t -> p (r t)"),
                 )
 
-        turns = [(c, b) for c in range(WEIGHT_GROUPS) for b in range(BATCHES)]
-        project_and_rotate(*turns[0])
-        done = 1
-        sort_unit(streamed_units[0])
+        x_codes = const.tile([P, BATCHES, PASSES, P], U32, name="x_codes", align_bytes=64)
+        x_scales = const.tile([P, BATCHES, PASSES, P], U8, name="x_scales", align_bytes=64)
+        words = unsorted_words(x_blocks[0])
+        for b in range(BATCHES):
+            grouped_tiles = regroup_block(words, (nc.scalar.copy, nc.scalar.copy))
+            if b + 1 < BATCHES:
+                words = sort_block(x_blocks[b + 1])
+            else:
+                sort_unit(streamed_units[0])
+            for pair in range(PASSES // 2):
+                passes = slice(2 * pair, 2 * pair + 2)
+                nc.vector.quantize_mx(
+                    out=x_codes[:, b, passes, :].rearrange("p g r -> p (g r)").bitcast(FP8X4),
+                    scales=x_scales[:, b, passes, :].rearrange("p g r -> p (g r)"),
+                    in_=grouped_tiles[pair][:].rearrange("p e r t -> p (e r t)"),
+                )
+            if b > 0:
+                project_and_rotate(0, b - 1)
+
+        turns = [(0, BATCHES - 1)] + [(c, b) for c in range(1, WEIGHT_GROUPS) for b in range(BATCHES)]
+        turns_behind = [1, 0] + [2] * (len(streamed_units) - 2)
+        done = 0
         for s, unit in enumerate(streamed_units):
             if s + LOADS_AHEAD < len(streamed_units):
                 start_load(streamed_units[s + LOADS_AHEAD])
             if s + 1 < len(streamed_units):
                 sort_unit(streamed_units[s + 1])
             quantise_unit(unit)
-            count = 1 if s == 1 else 2
-            for c, b in turns[done : done + count]:
+            for c, b in turns[done : done + turns_behind[s]]:
                 project_and_rotate(c, b)
-            done += count
+            done += turns_behind[s]
         for c, b in turns[done:]:
             project_and_rotate(c, b)

@@ -23,6 +23,9 @@ UNIT_ROWS = GROUP_ROWS // 2
 UNIT_BLOCKS = UNIT_ROWS // P
 GROUPS_PER_WEIGHT = CHANNELS // GROUP_ROWS
 WEIGHT_GROUPS = 2 * GROUPS_PER_WEIGHT
+UNSORTED_BATCHES = 2
+UNSORTED_UNITS = 2
+SORTS_AHEAD = 2
 LOADS_AHEAD = 6
 
 FLOPS = 2 * (BATCHES * P) * CHANNELS * (2 * CHANNELS)
@@ -99,7 +102,7 @@ def tile_attention_pa_kernel(tc, x, wq, wk, out_0, out_1):
         const = stack.enter_context(tc.tile_pool(name="const", bufs=1))
         block_pool = stack.enter_context(tc.tile_pool(name="block", bufs=BATCHES + GROUP_ROWS // P))
         unit_pool = stack.enter_context(tc.tile_pool(name="unit", bufs=LOADS_AHEAD + 1))
-        sorted_pool = stack.enter_context(tc.tile_pool(name="sorted", bufs=3))
+        sorted_pool = stack.enter_context(tc.tile_pool(name="sorted", bufs=SORTS_AHEAD + 1))
         sorted_block_pool = stack.enter_context(tc.tile_pool(name="sorted_block", bufs=2))
         grouped_pool = stack.enter_context(tc.tile_pool(name="grouped", bufs=2 * PASSES))
         weight_mx = stack.enter_context(tc.tile_pool(name="weight_mx", bufs=3))
@@ -171,7 +174,12 @@ def tile_attention_pa_kernel(tc, x, wq, wk, out_0, out_1):
             c, two = unit
             codes, scales = codes_of_group(c)
             columns = slice(two * UNIT_ROWS, (two + 1) * UNIT_ROWS)
-            planes = sorted_tiles[unit][:].rearrange("p u j k -> p (u j) k").bitcast(F32)
+            if unit in sorted_tiles:
+                planes = sorted_tiles[unit][:].bitcast(F32)
+                words = [[planes[:, u, j, :] for j in range(UNIT_BLOCKS)] for u in range(2)]
+            else:
+                raw_words = unit_tiles[unit][:].bitcast(F32)
+                words = [[raw_words[:, j, u::2] for j in range(UNIT_BLOCKS)] for u in range(2)]
             grouped_tiles = []
             for g in range(PASSES):
                 bank = transposed_pool.tile([P, 2, 2, P], F32, name="bank")
@@ -179,7 +187,7 @@ def tile_attention_pa_kernel(tc, x, wq, wk, out_0, out_1):
                     for j in range(2):
                         nc.tensor.transpose(
                             out=bank[:, u, j, :],
-                            in_=planes[:, 2 * u + j, g * P : (g + 1) * P],
+                            in_=words[u][j][:, g * P : (g + 1) * P],
                             identity=identity[:],
                         )
                 grouped = grouped_pool.tile([P, UNIT_ROWS, PACK], BF16, name="grouped", align_bytes=64)
@@ -192,7 +200,7 @@ def tile_attention_pa_kernel(tc, x, wq, wk, out_0, out_1):
                     in_=grouped_tiles[g][:].rearrange("p n t -> p (n t)"),
                 )
 
-        def project_and_rotate(c, b):
+        def project_and_rotate(c, b, parts=1):
             w_codes, w_scales = prepared[c]
             acc = acc_pool.tile([P, GROUP_ROWS], F32, name="acc")
             for g in range(PASSES):
@@ -208,21 +216,30 @@ def tile_attention_pa_kernel(tc, x, wq, wk, out_0, out_1):
             crossed = crossed_pool.tile([P, GROUP_ROWS], F32, name="crossed")
             even, odd = slice(0, UNIT_ROWS), slice(UNIT_ROWS, GROUP_ROWS)
             nc.scalar.activation(out=crossed[:, even], in_=acc[:, odd], func=ACT.Copy, scale=minus_sin_t)
-            nc.scalar.activation(out=crossed[:, odd], in_=acc[:, even], func=ACT.Copy, scale=sin_t)
+            if parts == 1:
+                nc.scalar.activation(out=crossed[:, odd], in_=acc[:, even], func=ACT.Copy, scale=sin_t)
+            else:
+                nc.vector.tensor_scalar(
+                    out=crossed[:, odd], in0=acc[:, even], scalar1=sin_t, scalar2=None, op0=ALU.mult
+                )
             rotated = rotated_pool.tile([P, UNIT_ROWS, 2], F32, name="rotated")
-            nc.vector.scalar_tensor_tensor(
-                out=rotated[:],
-                in0=acc[:].rearrange("p (two i) -> p i two", two=2),
-                scalar=cos_t,
-                in1=crossed[:].rearrange("p (two i) -> p i two", two=2),
-                op0=ALU.mult,
-                op1=ALU.add,
-            )
             first_channel = (c % GROUPS_PER_WEIGHT) * GROUP_ROWS
-            nc.sync.dma_start(
-                out=outputs[c // GROUPS_PER_WEIGHT][b, :, first_channel : first_channel + GROUP_ROWS],
-                in_=rotated[:].rearrange("p i two -> p (i two)"),
-            )
+            pairs = UNIT_ROWS // parts
+            for part in range(parts):
+                mine = slice(part * pairs, (part + 1) * pairs)
+                nc.vector.scalar_tensor_tensor(
+                    out=rotated[:, mine, :],
+                    in0=acc[:].rearrange("p (two i) -> p i two", two=2)[:, mine, :],
+                    scalar=cos_t,
+                    in1=crossed[:].rearrange("p (two i) -> p i two", two=2)[:, mine, :],
+                    op0=ALU.mult,
+                    op1=ALU.add,
+                )
+                channels = slice(first_channel + 2 * part * pairs, first_channel + 2 * (part + 1) * pairs)
+                nc.sync.dma_start(
+                    out=outputs[c // GROUPS_PER_WEIGHT][b, :, channels],
+                    in_=rotated[:, mine, :].rearrange("p i two -> p (i two)"),
+                )
 
         first_group_blocks = {}
         for two in range(2):
@@ -256,9 +273,7 @@ def tile_attention_pa_kernel(tc, x, wq, wk, out_0, out_1):
         for b in range(BATCHES):
             grouped_tiles = regroup_block(words, (nc.scalar.copy, nc.scalar.copy))
             if b + 1 < BATCHES:
-                words = sort_block(x_blocks[b + 1])
-            else:
-                sort_unit(streamed_units[0])
+                words = (unsorted_words if b + 1 < UNSORTED_BATCHES else sort_block)(x_blocks[b + 1])
             for pair in range(PASSES // 2):
                 passes = slice(2 * pair, 2 * pair + 2)
                 nc.vector.quantize_mx(
@@ -275,11 +290,12 @@ def tile_attention_pa_kernel(tc, x, wq, wk, out_0, out_1):
         for s, unit in enumerate(streamed_units):
             if s + LOADS_AHEAD < len(streamed_units):
                 start_load(streamed_units[s + LOADS_AHEAD])
-            if s + 1 < len(streamed_units):
-                sort_unit(streamed_units[s + 1])
+            if UNSORTED_UNITS <= s + SORTS_AHEAD < len(streamed_units):
+                sort_unit(streamed_units[s + SORTS_AHEAD])
             quantise_unit(unit)
             for c, b in turns[done : done + turns_behind[s]]:
                 project_and_rotate(c, b)
             done += turns_behind[s]
-        for c, b in turns[done:]:
+        for c, b in turns[done:-1]:
             project_and_rotate(c, b)
+        project_and_rotate(*turns[-1], parts=2)

@@ -117,19 +117,19 @@ def tile_attention_pa_kernel(tc, x, wq, wk, out_0, out_1):
         prepared = {}
 
         def load_block(view):
-            block = block_pool.tile([P, CHANNELS], BF16, name="block")
+            block = block_pool.tile([P, CHANNELS], BF16, name="block", align_bytes=256)
             nc.sync.dma_start(out=block[:], in_=view)
             return block
 
         def start_load(unit):
-            raw = unit_pool.tile([P, UNIT_BLOCKS, CHANNELS], BF16, name="raw")
+            raw = unit_pool.tile([P, UNIT_BLOCKS, CHANNELS], BF16, name="raw", align_bytes=256)
             nc.sync.dma_start(out=raw[:], in_=unit_views[unit])
             unit_tiles[unit] = raw
 
         def codes_of_group(c):
             if c not in prepared:
-                w_codes = weight_mx.tile([P, PASSES, GROUP_ROWS], U32, name="w_codes", align_bytes=64)
-                w_scales = weight_mx.tile([P, PASSES, GROUP_ROWS], U8, name="w_scales", align_bytes=64)
+                w_codes = weight_mx.tile([P, PASSES, GROUP_ROWS], U32, name="w_codes", align_bytes=256)
+                w_scales = weight_mx.tile([P, PASSES, GROUP_ROWS], U8, name="w_scales", align_bytes=256)
                 prepared[c] = (w_codes, w_scales)
             return prepared[c]
 
@@ -138,7 +138,7 @@ def tile_attention_pa_kernel(tc, x, wq, wk, out_0, out_1):
             return [words[:, u::2] for u in range(2)]
 
         def sort_block(block):
-            planes = sorted_block_pool.tile([P, 2, CHANNELS // 2], BF16, name="block_planes")
+            planes = sorted_block_pool.tile([P, 2, CHANNELS // 2], BF16, name="block_planes", align_bytes=256)
             nc.vector.tensor_copy(
                 out=planes[:].rearrange("p u (w e) -> p u w e", e=2),
                 in_=block[:].rearrange("p (w u e) -> p u w e", u=2, e=2),
@@ -157,13 +157,13 @@ def tile_attention_pa_kernel(tc, x, wq, wk, out_0, out_1):
                             in_=words[u][:, first_word : first_word + P],
                             identity=identity[:],
                         )
-                grouped = grouped_pool.tile([P, 2, P, PACK], BF16, name="grouped", align_bytes=64)
+                grouped = grouped_pool.tile([P, 2, P, PACK], BF16, name="grouped", align_bytes=256)
                 copy_engines[pair](out=grouped[:].bitcast(F32), in_=bank[:].rearrange("p e u r -> p e r u"))
                 grouped_tiles.append(grouped)
             return grouped_tiles
 
         def sort_unit(unit):
-            planes = sorted_pool.tile([P, 2, 2, CHANNELS // 2], BF16, name="planes")
+            planes = sorted_pool.tile([P, 2, 2, CHANNELS // 2], BF16, name="planes", align_bytes=256)
             nc.vector.tensor_copy(
                 out=planes[:].rearrange("p u j (w e) -> p u (j w) e", e=2),
                 in_=unit_tiles[unit][:].rearrange("p j (w u e) -> p u (j w) e", u=2, e=2),
@@ -190,7 +190,7 @@ def tile_attention_pa_kernel(tc, x, wq, wk, out_0, out_1):
                             in_=words[u][j][:, g * P : (g + 1) * P],
                             identity=identity[:],
                         )
-                grouped = grouped_pool.tile([P, UNIT_ROWS, PACK], BF16, name="grouped", align_bytes=64)
+                grouped = grouped_pool.tile([P, UNIT_ROWS, PACK], BF16, name="grouped", align_bytes=256)
                 nc.scalar.copy(out=grouped[:].bitcast(F32), in_=bank[:].rearrange("p u j r -> p (j r) u"))
                 grouped_tiles.append(grouped)
             for g in range(PASSES):
@@ -249,7 +249,7 @@ def tile_attention_pa_kernel(tc, x, wq, wk, out_0, out_1):
         for unit in streamed_units[:LOADS_AHEAD]:
             start_load(unit)
 
-        identity = const.tile([P, P], F32, name="identity")
+        identity = const.tile([P, P], F32, name="identity", align_bytes=256)
         make_identity(nc, identity[:])
 
         sin_t, minus_sin_t, cos_t = position_trig(nc, const)
@@ -267,8 +267,8 @@ def tile_attention_pa_kernel(tc, x, wq, wk, out_0, out_1):
                     in_=grouped_tiles[g // 2][:, g % 2].rearrange("p r t -> p (r t)"),
                 )
 
-        x_codes = const.tile([P, BATCHES, PASSES, P], U32, name="x_codes", align_bytes=64)
-        x_scales = const.tile([P, BATCHES, PASSES, P], U8, name="x_scales", align_bytes=64)
+        x_codes = const.tile([P, BATCHES, PASSES, P], U32, name="x_codes", align_bytes=256)
+        x_scales = const.tile([P, BATCHES, PASSES, P], U8, name="x_scales", align_bytes=256)
         words = unsorted_words(x_blocks[0])
         for b in range(BATCHES):
             grouped_tiles = regroup_block(words, (nc.scalar.copy, nc.scalar.copy))

@@ -23,8 +23,7 @@ UNIT_ROWS = GROUP_ROWS // 2
 UNIT_BLOCKS = UNIT_ROWS // P
 GROUPS_PER_WEIGHT = CHANNELS // GROUP_ROWS
 WEIGHT_GROUPS = 2 * GROUPS_PER_WEIGHT
-UNSORTED_BATCHES = 2
-UNSORTED_UNITS = 2
+UNSORTED_UNITS = 1
 SORTS_AHEAD = 2
 LOADS_AHEAD = 6
 
@@ -103,7 +102,6 @@ def tile_attention_pa_kernel(tc, x, wq, wk, out_0, out_1):
         block_pool = stack.enter_context(tc.tile_pool(name="block", bufs=BATCHES + GROUP_ROWS // P))
         unit_pool = stack.enter_context(tc.tile_pool(name="unit", bufs=LOADS_AHEAD + 1))
         sorted_pool = stack.enter_context(tc.tile_pool(name="sorted", bufs=SORTS_AHEAD + 1))
-        sorted_block_pool = stack.enter_context(tc.tile_pool(name="sorted_block", bufs=2))
         grouped_pool = stack.enter_context(tc.tile_pool(name="grouped", bufs=2 * PASSES))
         weight_mx = stack.enter_context(tc.tile_pool(name="weight_mx", bufs=3))
         crossed_pool = stack.enter_context(tc.tile_pool(name="crossed", bufs=4))
@@ -133,28 +131,17 @@ def tile_attention_pa_kernel(tc, x, wq, wk, out_0, out_1):
                 prepared[c] = (w_codes, w_scales)
             return prepared[c]
 
-        def unsorted_words(block):
+        def regroup_block(block, copy_engines):
             words = block[:].bitcast(F32)
-            return [words[:, u::2] for u in range(2)]
-
-        def sort_block(block):
-            planes = sorted_block_pool.tile([P, 2, CHANNELS // 2], BF16, name="block_planes", align_bytes=256)
-            nc.vector.tensor_copy(
-                out=planes[:].rearrange("p u (w e) -> p u w e", e=2),
-                in_=block[:].rearrange("p (w u e) -> p u w e", u=2, e=2),
-            )
-            return [planes[:, u, :].bitcast(F32) for u in range(2)]
-
-        def regroup_block(words, copy_engines):
             grouped_tiles = []
             for pair in range(PASSES // 2):
                 bank = transposed_pool.tile([P, 2, 2, P], F32, name="bank")
                 for e in range(2):
-                    first_word = (2 * pair + e) * P
+                    first_word = (2 * pair + e) * 2 * P
                     for u in range(2):
                         nc.tensor.transpose(
                             out=bank[:, e, u, :],
-                            in_=words[u][:, first_word : first_word + P],
+                            in_=words[:, first_word + u : first_word + 2 * P : 2],
                             identity=identity[:],
                         )
                 grouped = grouped_pool.tile([P, 2, P, PACK], BF16, name="grouped", align_bytes=256)
@@ -200,7 +187,7 @@ def tile_attention_pa_kernel(tc, x, wq, wk, out_0, out_1):
                     in_=grouped_tiles[g][:].rearrange("p n t -> p (n t)"),
                 )
 
-        def project_and_rotate(c, b, parts=1):
+        def project_and_rotate(c, b):
             w_codes, w_scales = prepared[c]
             acc = acc_pool.tile([P, GROUP_ROWS], F32, name="acc")
             for g in range(PASSES):
@@ -216,30 +203,21 @@ def tile_attention_pa_kernel(tc, x, wq, wk, out_0, out_1):
             crossed = crossed_pool.tile([P, GROUP_ROWS], F32, name="crossed")
             even, odd = slice(0, UNIT_ROWS), slice(UNIT_ROWS, GROUP_ROWS)
             nc.scalar.activation(out=crossed[:, even], in_=acc[:, odd], func=ACT.Copy, scale=minus_sin_t)
-            if parts == 1:
-                nc.scalar.activation(out=crossed[:, odd], in_=acc[:, even], func=ACT.Copy, scale=sin_t)
-            else:
-                nc.vector.tensor_scalar(
-                    out=crossed[:, odd], in0=acc[:, even], scalar1=sin_t, scalar2=None, op0=ALU.mult
-                )
+            nc.scalar.activation(out=crossed[:, odd], in_=acc[:, even], func=ACT.Copy, scale=sin_t)
             rotated = rotated_pool.tile([P, UNIT_ROWS, 2], F32, name="rotated")
+            nc.vector.scalar_tensor_tensor(
+                out=rotated[:],
+                in0=acc[:].rearrange("p (two i) -> p i two", two=2),
+                scalar=cos_t,
+                in1=crossed[:].rearrange("p (two i) -> p i two", two=2),
+                op0=ALU.mult,
+                op1=ALU.add,
+            )
             first_channel = (c % GROUPS_PER_WEIGHT) * GROUP_ROWS
-            pairs = UNIT_ROWS // parts
-            for part in range(parts):
-                mine = slice(part * pairs, (part + 1) * pairs)
-                nc.vector.scalar_tensor_tensor(
-                    out=rotated[:, mine, :],
-                    in0=acc[:].rearrange("p (two i) -> p i two", two=2)[:, mine, :],
-                    scalar=cos_t,
-                    in1=crossed[:].rearrange("p (two i) -> p i two", two=2)[:, mine, :],
-                    op0=ALU.mult,
-                    op1=ALU.add,
-                )
-                channels = slice(first_channel + 2 * part * pairs, first_channel + 2 * (part + 1) * pairs)
-                nc.sync.dma_start(
-                    out=outputs[c // GROUPS_PER_WEIGHT][b, :, channels],
-                    in_=rotated[:, mine, :].rearrange("p i two -> p (i two)"),
-                )
+            nc.sync.dma_start(
+                out=outputs[c // GROUPS_PER_WEIGHT][b, :, first_channel : first_channel + GROUP_ROWS],
+                in_=rotated[:].rearrange("p i two -> p (i two)"),
+            )
 
         first_group_blocks = {}
         for two in range(2):
@@ -257,7 +235,7 @@ def tile_attention_pa_kernel(tc, x, wq, wk, out_0, out_1):
         codes, scales = codes_of_group(0)
         for two, h in first_group_blocks:
             second_copy = nc.scalar.copy if h == 0 else nc.vector.tensor_copy
-            grouped_tiles = regroup_block(unsorted_words(first_group_blocks[two, h]), (nc.scalar.copy, second_copy))
+            grouped_tiles = regroup_block(first_group_blocks[two, h], (nc.scalar.copy, second_copy))
             first_column = two * UNIT_ROWS + h * P
             columns = slice(first_column, first_column + P)
             for g in range(PASSES):
@@ -269,11 +247,8 @@ def tile_attention_pa_kernel(tc, x, wq, wk, out_0, out_1):
 
         x_codes = const.tile([P, BATCHES, PASSES, P], U32, name="x_codes", align_bytes=256)
         x_scales = const.tile([P, BATCHES, PASSES, P], U8, name="x_scales", align_bytes=256)
-        words = unsorted_words(x_blocks[0])
         for b in range(BATCHES):
-            grouped_tiles = regroup_block(words, (nc.scalar.copy, nc.scalar.copy))
-            if b + 1 < BATCHES:
-                words = (unsorted_words if b + 1 < UNSORTED_BATCHES else sort_block)(x_blocks[b + 1])
+            grouped_tiles = regroup_block(x_blocks[b], (nc.scalar.copy, nc.scalar.copy))
             for pair in range(PASSES // 2):
                 passes = slice(2 * pair, 2 * pair + 2)
                 nc.vector.quantize_mx(
@@ -281,21 +256,22 @@ def tile_attention_pa_kernel(tc, x, wq, wk, out_0, out_1):
                     scales=x_scales[:, b, passes, :].rearrange("p g r -> p (g r)"),
                     in_=grouped_tiles[pair][:].rearrange("p e r t -> p (e r t)"),
                 )
-            if b > 0:
-                project_and_rotate(0, b - 1)
+            if b == 2:
+                project_and_rotate(0, 0)
+        for unit in streamed_units[UNSORTED_UNITS:SORTS_AHEAD]:
+            sort_unit(unit)
 
-        turns = [(0, BATCHES - 1)] + [(c, b) for c in range(1, WEIGHT_GROUPS) for b in range(BATCHES)]
-        turns_behind = [1, 0] + [2] * (len(streamed_units) - 2)
-        done = 0
+        turns = [(c, b) for c in range(WEIGHT_GROUPS) for b in range(BATCHES)]
+        done = 1
         for s, unit in enumerate(streamed_units):
             if s + LOADS_AHEAD < len(streamed_units):
                 start_load(streamed_units[s + LOADS_AHEAD])
-            if UNSORTED_UNITS <= s + SORTS_AHEAD < len(streamed_units):
+            if s + SORTS_AHEAD < len(streamed_units):
                 sort_unit(streamed_units[s + SORTS_AHEAD])
             quantise_unit(unit)
-            for c, b in turns[done : done + turns_behind[s]]:
+            count = 1 if s < 3 else 2
+            for c, b in turns[done : done + count]:
                 project_and_rotate(c, b)
-            done += turns_behind[s]
-        for c, b in turns[done:-1]:
+            done += count
+        for c, b in turns[done:]:
             project_and_rotate(c, b)
-        project_and_rotate(*turns[-1], parts=2)

@@ -187,37 +187,47 @@ def tile_attention_pa_kernel(tc, x, wq, wk, out_0, out_1):
                     in_=grouped_tiles[g][:].rearrange("p n t -> p (n t)"),
                 )
 
-        def project_and_rotate(c, b):
+        def project_and_rotate(c, b, parts=1):
             w_codes, w_scales = prepared[c]
-            acc = acc_pool.tile([P, GROUP_ROWS], F32, name="acc")
-            for g in range(PASSES):
-                nc.tensor.matmul_mx(
-                    out=acc[:],
-                    lhsT=x_codes[:, b, g, :].bitcast(FP8X4),
-                    lhsT_scale=x_scales[:, b, g, :],
-                    rhs=w_codes[:, g, :].bitcast(FP8X4),
-                    rhs_scale=w_scales[:, g, :],
-                    start=(g == 0),
-                    stop=(g == PASSES - 1),
+            pairs = UNIT_ROWS // parts
+            for part in range(parts):
+                acc = acc_pool.tile([P, 2, pairs], F32, name="acc")
+                column_runs = (
+                    [(acc[:].rearrange("p two i -> p (two i)"), slice(0, GROUP_ROWS))]
+                    if parts == 1
+                    else [
+                        (acc[:, two, :], slice(two * UNIT_ROWS + part * pairs, two * UNIT_ROWS + (part + 1) * pairs))
+                        for two in range(2)
+                    ]
                 )
-            crossed = crossed_pool.tile([P, GROUP_ROWS], F32, name="crossed")
-            even, odd = slice(0, UNIT_ROWS), slice(UNIT_ROWS, GROUP_ROWS)
-            nc.scalar.activation(out=crossed[:, even], in_=acc[:, odd], func=ACT.Copy, scale=minus_sin_t)
-            nc.scalar.activation(out=crossed[:, odd], in_=acc[:, even], func=ACT.Copy, scale=sin_t)
-            rotated = rotated_pool.tile([P, UNIT_ROWS, 2], F32, name="rotated")
-            nc.vector.scalar_tensor_tensor(
-                out=rotated[:],
-                in0=acc[:].rearrange("p (two i) -> p i two", two=2),
-                scalar=cos_t,
-                in1=crossed[:].rearrange("p (two i) -> p i two", two=2),
-                op0=ALU.mult,
-                op1=ALU.add,
-            )
-            first_channel = (c % GROUPS_PER_WEIGHT) * GROUP_ROWS
-            nc.sync.dma_start(
-                out=outputs[c // GROUPS_PER_WEIGHT][b, :, first_channel : first_channel + GROUP_ROWS],
-                in_=rotated[:].rearrange("p i two -> p (i two)"),
-            )
+                for sums, columns in column_runs:
+                    for g in range(PASSES):
+                        nc.tensor.matmul_mx(
+                            out=sums,
+                            lhsT=x_codes[:, b, g, :].bitcast(FP8X4),
+                            lhsT_scale=x_scales[:, b, g, :],
+                            rhs=w_codes[:, g, columns].bitcast(FP8X4),
+                            rhs_scale=w_scales[:, g, columns],
+                            start=(g == 0),
+                            stop=(g == PASSES - 1),
+                        )
+                crossed = crossed_pool.tile([P, 2, pairs], F32, name="crossed")
+                nc.scalar.activation(out=crossed[:, 0, :], in_=acc[:, 1, :], func=ACT.Copy, scale=minus_sin_t)
+                nc.scalar.activation(out=crossed[:, 1, :], in_=acc[:, 0, :], func=ACT.Copy, scale=sin_t)
+                rotated = rotated_pool.tile([P, pairs, 2], F32, name="rotated")
+                nc.vector.scalar_tensor_tensor(
+                    out=rotated[:],
+                    in0=acc[:].rearrange("p two i -> p i two"),
+                    scalar=cos_t,
+                    in1=crossed[:].rearrange("p two i -> p i two"),
+                    op0=ALU.mult,
+                    op1=ALU.add,
+                )
+                first_channel = (c % GROUPS_PER_WEIGHT) * GROUP_ROWS + part * 2 * pairs
+                nc.sync.dma_start(
+                    out=outputs[c // GROUPS_PER_WEIGHT][b, :, first_channel : first_channel + 2 * pairs],
+                    in_=rotated[:].rearrange("p i two -> p (i two)"),
+                )
 
         first_group_blocks = {}
         for two in range(2):
@@ -273,5 +283,6 @@ def tile_attention_pa_kernel(tc, x, wq, wk, out_0, out_1):
             for c, b in turns[done : done + count]:
                 project_and_rotate(c, b)
             done += count
-        for c, b in turns[done:]:
+        for c, b in turns[done:-1]:
             project_and_rotate(c, b)
+        project_and_rotate(*turns[-1], parts=2)

@@ -187,23 +187,37 @@ def tile_attention_pa_kernel(tc, x, wq, wk, out_0, out_1):
                     in_=grouped_tiles[g][:].rearrange("p n t -> p (n t)"),
                 )
 
-        def project_and_rotate(c, b, parts=1):
+        def project(turns):
+            accs = []
+            for c, b in turns:
+                acc = acc_pool.tile([P, 2, UNIT_ROWS], F32, name="acc")
+                accs.append(acc)
+            for g in range(PASSES):
+                for (c, b), acc in zip(turns, accs):
+                    w_codes, w_scales = prepared[c]
+                    nc.tensor.matmul_mx(
+                        out=acc[:].rearrange("p two i -> p (two i)"),
+                        lhsT=x_codes[:, b, g, :].bitcast(FP8X4),
+                        lhsT_scale=x_scales[:, b, g, :],
+                        rhs=w_codes[:, g, :].bitcast(FP8X4),
+                        rhs_scale=w_scales[:, g, :],
+                        start=(g == 0),
+                        stop=(g == PASSES - 1),
+                    )
+            for (c, b), acc in zip(turns, accs):
+                rotate(c, b, acc, UNIT_ROWS, 0)
+
+        def project_in_parts(c, b, parts):
             w_codes, w_scales = prepared[c]
             pairs = UNIT_ROWS // parts
             for part in range(parts):
                 acc = acc_pool.tile([P, 2, pairs], F32, name="acc")
-                column_runs = (
-                    [(acc[:].rearrange("p two i -> p (two i)"), slice(0, GROUP_ROWS))]
-                    if parts == 1
-                    else [
-                        (acc[:, two, :], slice(two * UNIT_ROWS + part * pairs, two * UNIT_ROWS + (part + 1) * pairs))
-                        for two in range(2)
-                    ]
-                )
-                for sums, columns in column_runs:
+                for two in range(2):
+                    first_column = two * UNIT_ROWS + part * pairs
+                    columns = slice(first_column, first_column + pairs)
                     for g in range(PASSES):
                         nc.tensor.matmul_mx(
-                            out=sums,
+                            out=acc[:, two, :],
                             lhsT=x_codes[:, b, g, :].bitcast(FP8X4),
                             lhsT_scale=x_scales[:, b, g, :],
                             rhs=w_codes[:, g, columns].bitcast(FP8X4),
@@ -211,23 +225,26 @@ def tile_attention_pa_kernel(tc, x, wq, wk, out_0, out_1):
                             start=(g == 0),
                             stop=(g == PASSES - 1),
                         )
-                crossed = crossed_pool.tile([P, 2, pairs], F32, name="crossed")
-                nc.scalar.activation(out=crossed[:, 0, :], in_=acc[:, 1, :], func=ACT.Copy, scale=minus_sin_t)
-                nc.scalar.activation(out=crossed[:, 1, :], in_=acc[:, 0, :], func=ACT.Copy, scale=sin_t)
-                rotated = rotated_pool.tile([P, pairs, 2], F32, name="rotated")
-                nc.vector.scalar_tensor_tensor(
-                    out=rotated[:],
-                    in0=acc[:].rearrange("p two i -> p i two"),
-                    scalar=cos_t,
-                    in1=crossed[:].rearrange("p two i -> p i two"),
-                    op0=ALU.mult,
-                    op1=ALU.add,
-                )
-                first_channel = (c % GROUPS_PER_WEIGHT) * GROUP_ROWS + part * 2 * pairs
-                nc.sync.dma_start(
-                    out=outputs[c // GROUPS_PER_WEIGHT][b, :, first_channel : first_channel + 2 * pairs],
-                    in_=rotated[:].rearrange("p i two -> p (i two)"),
-                )
+                rotate(c, b, acc, pairs, part)
+
+        def rotate(c, b, acc, pairs, part):
+            crossed = crossed_pool.tile([P, 2, pairs], F32, name="crossed")
+            nc.scalar.activation(out=crossed[:, 0, :], in_=acc[:, 1, :], func=ACT.Copy, scale=minus_sin_t)
+            nc.scalar.activation(out=crossed[:, 1, :], in_=acc[:, 0, :], func=ACT.Copy, scale=sin_t)
+            rotated = rotated_pool.tile([P, pairs, 2], F32, name="rotated")
+            nc.vector.scalar_tensor_tensor(
+                out=rotated[:],
+                in0=acc[:].rearrange("p two i -> p i two"),
+                scalar=cos_t,
+                in1=crossed[:].rearrange("p two i -> p i two"),
+                op0=ALU.mult,
+                op1=ALU.add,
+            )
+            first_channel = (c % GROUPS_PER_WEIGHT) * GROUP_ROWS + part * 2 * pairs
+            nc.sync.dma_start(
+                out=outputs[c // GROUPS_PER_WEIGHT][b, :, first_channel : first_channel + 2 * pairs],
+                in_=rotated[:].rearrange("p i two -> p (i two)"),
+            )
 
         first_group_blocks = {}
         for two in range(2):
@@ -267,7 +284,7 @@ def tile_attention_pa_kernel(tc, x, wq, wk, out_0, out_1):
                     in_=grouped_tiles[pair][:].rearrange("p e r t -> p (e r t)"),
                 )
             if b == 2:
-                project_and_rotate(0, 0)
+                project([(0, 0)])
         for unit in streamed_units[UNSORTED_UNITS:SORTS_AHEAD]:
             sort_unit(unit)
 
@@ -280,9 +297,8 @@ def tile_attention_pa_kernel(tc, x, wq, wk, out_0, out_1):
                 sort_unit(streamed_units[s + SORTS_AHEAD])
             quantise_unit(unit)
             count = 1 if s < 3 else 2
-            for c, b in turns[done : done + count]:
-                project_and_rotate(c, b)
+            project(turns[done : done + count])
             done += count
-        for c, b in turns[done:-1]:
-            project_and_rotate(c, b)
-        project_and_rotate(*turns[-1], parts=2)
+        for turn in turns[done:-1]:
+            project([turn])
+        project_in_parts(*turns[-1], parts=2)

import math
from contextlib import ExitStack

import concourse.mybir as mybir
from concourse.masks import make_identity

F32 = mybir.dt.float32
BF16 = mybir.dt.bfloat16
I32 = mybir.dt.int32
U32 = mybir.dt.uint32
U8 = mybir.dt.uint8
FP8X4 = mybir.dt.float8_e4m3fn_x4
ALU = mybir.AluOpType
ACT = mybir.ActivationFunctionType

P = 128
BATCHES = 4
CHANNELS = 2048
PACK = 4
PASSES = CHANNELS // (P * PACK)
GROUP_ROWS = 512
UNIT_ROWS = GROUP_ROWS // 2
UNIT_BLOCKS = UNIT_ROWS // P
GROUPS_PER_WEIGHT = CHANNELS // GROUP_ROWS
WEIGHT_GROUPS = 2 * GROUPS_PER_WEIGHT
UNSORTED_UNITS = 1
SORTS_AHEAD = 2
LOADS_AHEAD = 6

FLOPS = 2 * (BATCHES * P) * CHANNELS * (2 * CHANNELS)

TWO_PI = 2.0 * math.pi
TWO_PI_HIGH = 6.28125
TWO_PI_MID = int((TWO_PI - TWO_PI_HIGH) * 2**25) / 2**25
TWO_PI_LOW = TWO_PI - TWO_PI_HIGH - TWO_PI_MID
HALF_PI_HIGH = int(0.5 * math.pi * 2**20) / 2**20
HALF_PI_LOW = 0.5 * math.pi - HALF_PI_HIGH
ROUND_TO_WHOLE = 1.5 * 2**23


def position_trig(nc, pool):
    position_int = pool.tile([P, 1], I32, name="position_int")
    nc.gpsimd.iota(position_int[:], pattern=[[0, 1]], base=0, channel_multiplier=1)
    position = pool.tile([P, 1], F32, name="position")
    nc.vector.tensor_copy(out=position[:], in_=position_int[:])

    shifted = pool.tile([P, 1], F32, name="shifted")
    nc.vector.tensor_scalar(
        out=shifted[:], in0=position[:], scalar1=1.0 / TWO_PI, scalar2=ROUND_TO_WHOLE, op0=ALU.mult, op1=ALU.add
    )
    turns = pool.tile([P, 1], F32, name="turns")
    nc.vector.tensor_scalar(out=turns[:], in0=shifted[:], scalar1=ROUND_TO_WHOLE, scalar2=None, op0=ALU.subtract)

    angles = pool.tile([P, 2], F32, name="angles")
    less_high = pool.tile([P, 1], F32, name="less_high")
    less_mid = pool.tile([P, 1], F32, name="less_mid")
    nc.vector.scalar_tensor_tensor(
        out=less_high[:], in0=turns[:], scalar=-TWO_PI_HIGH, in1=position[:], op0=ALU.mult, op1=ALU.add
    )
    nc.vector.scalar_tensor_tensor(
        out=less_mid[:], in0=turns[:], scalar=-TWO_PI_MID, in1=less_high[:], op0=ALU.mult, op1=ALU.add
    )
    nc.vector.scalar_tensor_tensor(
        out=angles[:, 0:1], in0=turns[:], scalar=-TWO_PI_LOW, in1=less_mid[:], op0=ALU.mult, op1=ALU.add
    )
    magnitude = pool.tile([P, 1], F32, name="magnitude")
    nc.vector.scalar_tensor_tensor(
        out=magnitude[:], in0=angles[:, 0:1], scalar=-1.0, in1=angles[:, 0:1], op0=ALU.mult, op1=ALU.max
    )
    nc.vector.tensor_scalar(
        out=angles[:, 1:2],
        in0=magnitude[:],
        scalar1=HALF_PI_HIGH,
        scalar2=HALF_PI_LOW,
        op0=ALU.subtract,
        op1=ALU.subtract,
    )

    sines = pool.tile([P, 2], F32, name="sines")
    nc.scalar.activation(out=sines[:], in_=angles[:], func=ACT.Sin)
    negated = pool.tile([P, 2], F32, name="negated")
    nc.vector.tensor_scalar(out=negated[:], in0=sines[:], scalar1=-1.0, scalar2=None, op0=ALU.mult)
    return sines[:, 0:1], negated[:, 0:1], negated[:, 1:2]


def tile_attention_pa_kernel(tc, x, wq, wk, out_0, out_1):
    nc = tc.nc

    unit_views = {}
    for c in range(WEIGHT_GROUPS):
        first_row = (c % GROUPS_PER_WEIGHT) * GROUP_ROWS
        rows = (wq, wk)[c // GROUPS_PER_WEIGHT][first_row : first_row + GROUP_ROWS, :]
        by_parity = rows.rearrange("(h r two) k -> two r h k", h=UNIT_BLOCKS, two=2)
        for two in range(2):
            unit_views[c, two] = by_parity[two]
    streamed_units = [unit for unit in unit_views if unit[0] > 0]

    outputs = [out.rearrange("b t h d -> b t (h d)") for out in (out_0, out_1)]

    with ExitStack() as stack:
        const = stack.enter_context(tc.tile_pool(name="const", bufs=1))
        block_pool = stack.enter_context(tc.tile_pool(name="block", bufs=BATCHES + GROUP_ROWS // P))
        unit_pool = stack.enter_context(tc.tile_pool(name="unit", bufs=LOADS_AHEAD + 1))
        sorted_pool = stack.enter_context(tc.tile_pool(name="sorted", bufs=SORTS_AHEAD + 1))
        grouped_pool = stack.enter_context(tc.tile_pool(name="grouped", bufs=2 * PASSES))
        weight_mx = stack.enter_context(tc.tile_pool(name="weight_mx", bufs=3))
        crossed_pool = stack.enter_context(tc.tile_pool(name="crossed", bufs=4))
        rotated_pool = stack.enter_context(tc.tile_pool(name="rotated", bufs=6))
        transposed_pool = stack.enter_context(tc.psum_pool(name="transposed", bufs=4))
        acc_pool = stack.enter_context(tc.psum_pool(name="acc", bufs=4))
        stack.enter_context(tc.manual_schedule())

        unit_tiles = {}
        sorted_tiles = {}
        prepared = {}

        def load_block(view):
            block = block_pool.tile([P, CHANNELS], BF16, name="block", align_bytes=256)
            nc.sync.dma_start(out=block[:], in_=view)
            return block

        def start_load(unit):
            raw = unit_pool.tile([P, UNIT_BLOCKS, CHANNELS], BF16, name="raw", align_bytes=256)
            nc.sync.dma_start(out=raw[:], in_=unit_views[unit])
            unit_tiles[unit] = raw

        def codes_of_group(c):
            if c not in prepared:
                w_codes = weight_mx.tile([P, PASSES, GROUP_ROWS], U32, name="w_codes", align_bytes=256)
                w_scales = weight_mx.tile([P, PASSES, GROUP_ROWS], U8, name="w_scales", align_bytes=256)
                prepared[c] = (w_codes, w_scales)
            return prepared[c]

        def regroup_block(block, copy_engines):
            words = block[:].bitcast(F32)
            grouped_tiles = []
            for pair in range(PASSES // 2):
                bank = transposed_pool.tile([P, 2, 2, P], F32, name="bank")
                for e in range(2):
                    first_word = (2 * pair + e) * 2 * P
                    for u in range(2):
                        nc.tensor.transpose(
                            out=bank[:, e, u, :],
                            in_=words[:, first_word + u : first_word + 2 * P : 2],
                            identity=identity[:],
                        )
                grouped = grouped_pool.tile([P, 2, P, PACK], BF16, name="grouped", align_bytes=256)
                copy_engines[pair](out=grouped[:].bitcast(F32), in_=bank[:].rearrange("p e u r -> p e r u"))
                grouped_tiles.append(grouped)
            return grouped_tiles

        def sort_unit(unit):
            planes = sorted_pool.tile([P, 2, 2, CHANNELS // 2], BF16, name="planes", align_bytes=256)
            nc.vector.tensor_copy(
                out=planes[:].rearrange("p u j (w e) -> p u (j w) e", e=2),
                in_=unit_tiles[unit][:].rearrange("p j (w u e) -> p u (j w) e", u=2, e=2),
            )
            sorted_tiles[unit] = planes

        def quantise_unit(unit):
            c, two = unit
            codes, scales = codes_of_group(c)
            columns = slice(two * UNIT_ROWS, (two + 1) * UNIT_ROWS)
            if unit in sorted_tiles:
                planes = sorted_tiles[unit][:].bitcast(F32)
                words = [[planes[:, u, j, :] for j in range(UNIT_BLOCKS)] for u in range(2)]
            else:
                raw_words = unit_tiles[unit][:].bitcast(F32)
                words = [[raw_words[:, j, u::2] for j in range(UNIT_BLOCKS)] for u in range(2)]
            grouped_tiles = []
            for g in range(PASSES):
                bank = transposed_pool.tile([P, 2, 2, P], F32, name="bank")
                for u in range(2):
                    for j in range(2):
                        nc.tensor.transpose(
                            out=bank[:, u, j, :],
                            in_=words[u][j][:, g * P : (g + 1) * P],
                            identity=identity[:],
                        )
                grouped = grouped_pool.tile([P, UNIT_ROWS, PACK], BF16, name="grouped", align_bytes=256)
                nc.scalar.copy(out=grouped[:].bitcast(F32), in_=bank[:].rearrange("p u j r -> p (j r) u"))
                grouped_tiles.append(grouped)
            for g in range(PASSES):
                nc.vector.quantize_mx(
                    out=codes[:, g, columns].bitcast(FP8X4),
                    scales=scales[:, g, columns],
                    in_=grouped_tiles[g][:].rearrange("p n t -> p (n t)"),
                )

        def project(turns):
            accs = []
            for c, b in turns:
                acc = acc_pool.tile([P, 2, UNIT_ROWS], F32, name="acc")
                accs.append(acc)
            for g in range(PASSES):
                for (c, b), acc in zip(turns, accs):
                    w_codes, w_scales = prepared[c]
                    nc.tensor.matmul_mx(
                        out=acc[:].rearrange("p two i -> p (two i)"),
                        lhsT=x_codes[:, b, g, :].bitcast(FP8X4),
                        lhsT_scale=x_scales[:, b, g, :],
                        rhs=w_codes[:, g, :].bitcast(FP8X4),
                        rhs_scale=w_scales[:, g, :],
                        start=(g == 0),
                        stop=(g == PASSES - 1),
                    )
            for (c, b), acc in zip(turns, accs):
                rotate(c, b, acc, UNIT_ROWS, 0)

        def project_in_parts(c, b, parts):
            w_codes, w_scales = prepared[c]
            pairs = UNIT_ROWS // parts
            for part in range(parts):
                acc = acc_pool.tile([P, 2, pairs], F32, name="acc")
                for two in range(2):
                    first_column = two * UNIT_ROWS + part * pairs
                    columns = slice(first_column, first_column + pairs)
                    for g in range(PASSES):
                        nc.tensor.matmul_mx(
                            out=acc[:, two, :],
                            lhsT=x_codes[:, b, g, :].bitcast(FP8X4),
                            lhsT_scale=x_scales[:, b, g, :],
                            rhs=w_codes[:, g, columns].bitcast(FP8X4),
                            rhs_scale=w_scales[:, g, columns],
                            start=(g == 0),
                            stop=(g == PASSES - 1),
                        )
                rotate(c, b, acc, pairs, part)

        def rotate(c, b, acc, pairs, part):
            crossed = crossed_pool.tile([P, 2, pairs], F32, name="crossed")
            nc.scalar.activation(out=crossed[:, 0, :], in_=acc[:, 1, :], func=ACT.Copy, scale=minus_sin_t)
            nc.scalar.activation(out=crossed[:, 1, :], in_=acc[:, 0, :], func=ACT.Copy, scale=sin_t)
            rotated = rotated_pool.tile([P, pairs, 2], F32, name="rotated")
            nc.vector.scalar_tensor_tensor(
                out=rotated[:],
                in0=acc[:].rearrange("p two i -> p i two"),
                scalar=cos_t,
                in1=crossed[:].rearrange("p two i -> p i two"),
                op0=ALU.mult,
                op1=ALU.add,
            )
            first_channel = (c % GROUPS_PER_WEIGHT) * GROUP_ROWS + part * 2 * pairs
            nc.sync.dma_start(
                out=outputs[c // GROUPS_PER_WEIGHT][b, :, first_channel : first_channel + 2 * pairs],
                in_=rotated[:].rearrange("p i two -> p (i two)"),
            )

        first_group_blocks = {}
        for two in range(2):
            for h in range(UNIT_BLOCKS):
                first_group_blocks[two, h] = load_block(unit_views[0, two][:, h, :])
        x_blocks = [load_block(x[b]) for b in range(BATCHES)]
        for unit in streamed_units[:LOADS_AHEAD]:
            start_load(unit)

        identity = const.tile([P, P], F32, name="identity", align_bytes=256)
        make_identity(nc, identity[:])

        sin_t, minus_sin_t, cos_t = position_trig(nc, const)

        codes, scales = codes_of_group(0)
        for two, h in first_group_blocks:
            second_copy = nc.scalar.copy if h == 0 else nc.vector.tensor_copy
            grouped_tiles = regroup_block(first_group_blocks[two, h], (nc.scalar.copy, second_copy))
            first_column = two * UNIT_ROWS + h * P
            columns = slice(first_column, first_column + P)
            for g in range(PASSES):
                nc.vector.quantize_mx(
                    out=codes[:, g, columns].bitcast(FP8X4),
                    scales=scales[:, g, columns],
                    in_=grouped_tiles[g // 2][:, g % 2].rearrange("p r t -> p (r t)"),
                )

        x_codes = const.tile([P, BATCHES, PASSES, P], U32, name="x_codes", align_bytes=256)
        x_scales = const.tile([P, BATCHES, PASSES, P], U8, name="x_scales", align_bytes=256)
        for b in range(BATCHES):
            grouped_tiles = regroup_block(x_blocks[b], (nc.scalar.copy, nc.scalar.copy))
            for pair in range(PASSES // 2):
                passes = slice(2 * pair, 2 * pair + 2)
                nc.vector.quantize_mx(
                    out=x_codes[:, b, passes, :].rearrange("p g r -> p (g r)").bitcast(FP8X4),
                    scales=x_scales[:, b, passes, :].rearrange("p g r -> p (g r)"),
                    in_=grouped_tiles[pair][:].rearrange("p e r t -> p (e r t)"),
                )
            if b == 2:
                project([(0, 0)])
        for unit in streamed_units[UNSORTED_UNITS:SORTS_AHEAD]:
            sort_unit(unit)

        turns = [(c, b) for c in range(WEIGHT_GROUPS) for b in range(BATCHES)]
        done = 1
        for s, unit in enumerate(streamed_units):
            if s + LOADS_AHEAD < len(streamed_units):
                start_load(streamed_units[s + LOADS_AHEAD])
            if s + SORTS_AHEAD < len(streamed_units):
                sort_unit(streamed_units[s + SORTS_AHEAD])
            quantise_unit(unit)
            count = 1 if s < 3 else 2
            project(turns[done : done + count])
            done += count
        for turn in turns[done:-1]:
            project([turn])
        project_in_parts(*turns[-1], parts=2)
